import numpy as np
import ml_dtypes


def mxq(x, axis, fmt="e4m3"):
    dtype, down = {"e4m3": (ml_dtypes.float8_e4m3fn, 7), "e5m2": (ml_dtypes.float8_e5m2, 14)}[fmt]
    v = np.moveaxis(np.asarray(x, np.float32).astype(ml_dtypes.bfloat16).astype(np.float64), axis, -1)
    blocks = v.reshape(v.shape[:-1] + (-1, 32))
    amax = np.abs(blocks).max(-1, keepdims=True)
    byte = np.maximum(np.where(amax > 0, np.frexp(amax)[1] - 1 + 127, 0) - down, 1)
    scale = np.exp2(byte - 127.0)
    codes = (blocks / scale).astype(np.float32).astype(dtype).astype(np.float64)
    return np.moveaxis((codes * scale).reshape(v.shape), -1, axis)


WIDE = False


def mx_kscale(k):
    if not WIDE:
        return np.ones(k)
    levels = np.array([10, -10, 5, -5, 0])
    a = np.random.permutation(np.resize(levels, k // 512 * 4)).reshape(k // 512, 4)
    idx = np.arange(k)
    return np.exp2(a[idx // 512, idx % 128 // 32])


BF16 = ml_dtypes.bfloat16


def bf(x):
    return np.asarray(x, np.float32).astype(BF16)


def f64(x):
    return np.asarray(x).astype(np.float64)


E2M1 = np.array([0.0, 0.5, 1.0, 1.5, 2.0, 3.0, 4.0, 6.0, -0.0, -0.5, -1.0, -1.5, -2.0, -3.0, -4.0, -6.0])


def pack_weight(w, fmt):
    k, n = w.shape
    w = f64(bf(w)).reshape(k // 32, 32, n)
    amax = np.abs(w).max(1)
    if fmt == "e4m3":
        byte = np.frexp(amax)[1] - 1 + 127 - 7
    else:
        mant, ex = np.frexp(amax / 6.0)
        byte = np.where(mant > 0.5, ex, ex - 1) + 127
    byte = np.clip(np.where(amax > 0, byte, 1), 1, 254)
    scaled = (w * np.exp2(127.0 - byte)[:, None, :]).reshape(k, n).astype(np.float32)
    by_word = np.ascontiguousarray(scaled.reshape(k // 512, 128, 4, n).transpose(0, 1, 3, 2))
    if fmt == "e4m3":
        words = by_word.astype(ml_dtypes.float8_e4m3fn).view(np.uint8)
    else:
        c = by_word.astype(ml_dtypes.float4_e2m1fn).view(np.uint8) & 0xF
        words = c[..., 0::2] | (c[..., 1::2] << 4)
    return np.ascontiguousarray(words), np.ascontiguousarray(byte.astype(np.uint8).reshape(k // 512, 16, n))


def unpack_weight(words, scales, fmt):
    g, p, n, _ = words.shape
    if fmt == "e4m3":
        vals = np.ascontiguousarray(words).view(ml_dtypes.float8_e4m3fn).astype(np.float64)
    else:
        nib = np.empty((g, p, n, 4), np.uint8)
        nib[..., 0::2] = words & 0xF
        nib[..., 1::2] = words >> 4
        vals = E2M1[nib]
    vals = vals * np.repeat(np.exp2(scales.astype(np.float64) - 127.0), 8, axis=1)[..., None]
    return vals.transpose(0, 1, 3, 2).reshape(g * 512, n)

def pack4(w):
    words, scales = pack_weight(w, "e2m1")
    return words.reshape(words.shape[0], 128, -1), scales


def unpack4(words, scales):
    return unpack_weight(words.reshape(words.shape[0], 128, -1, 2), scales, "e2m1")


B, I, H = 8192, 1024, 128


def sigmoid(v):
    return 1.0 / (1.0 + np.exp(-v))


def setup_inputs():
    s = mx_kscale(I)
    input_ = bf(np.random.standard_normal((B, I)) * s)
    c_input = bf(np.random.standard_normal((B, 1, H)))
    h_0 = bf(np.random.standard_normal((B, H)))
    weight_ih_words, weight_ih_scales = pack4(np.random.standard_normal((I, 3 * H)) / np.sqrt(I) / s[:, None])
    weight_hh = bf(np.random.standard_normal((H, 3 * H)) / np.sqrt(H))
    alpha_weight_ih_words, alpha_weight_ih_scales = pack4(np.random.standard_normal((I, H)) / np.sqrt(I) / s[:, None])
    alpha_weight_hh = bf(np.random.standard_normal((H, H)) / np.sqrt(H))
    bias = bf(np.random.standard_normal(3 * H) * 0.5)
    alpha_bias = bf(np.random.standard_normal(H) * 0.5)
    return {
        "input_": input_,
        "c_input": c_input,
        "h_0": h_0,
        "weight_ih_words": weight_ih_words,
        "weight_ih_scales": weight_ih_scales,
        "weight_hh": weight_hh,
        "alpha_weight_ih_words": alpha_weight_ih_words,
        "alpha_weight_ih_scales": alpha_weight_ih_scales,
        "alpha_weight_hh": alpha_weight_hh,
        "bias": bias,
        "alpha_bias": alpha_bias,
    }


def reference(input_, c_input, h_0, weight_ih_words, weight_ih_scales, weight_hh, alpha_weight_ih_words, alpha_weight_ih_scales, alpha_weight_hh, bias, alpha_bias):
    xq = mxq(f64(input_), 1, "e4m3")
    wh_b = f64(h_0) @ f64(weight_hh) + f64(bias)
    wi = xq @ unpack4(weight_ih_words, weight_ih_scales)
    pre = wh_b + wi
    i_gate = sigmoid(pre[:, :H])
    o_gate = sigmoid(pre[:, H:2 * H])
    g = np.tanh(pre[:, 2 * H:])
    c_in = f64(c_input)[:, 0, :]
    alpha = sigmoid((xq @ unpack4(alpha_weight_ih_words, alpha_weight_ih_scales)) + f64(alpha_bias) + c_in @ f64(alpha_weight_hh))
    e_i = np.exp(i_gate)
    e_a = np.exp(alpha)
    denom = e_i + e_a
    w_i = e_i / denom
    w_a = e_a / denom
    c_1 = w_i * g + w_a * c_in
    h_1 = o_gate * np.tanh(c_1)
    return (h_1, c_1)

@@ -1,0 +1,306 @@
+from contextlib import ExitStack
+
+import concourse.mybir as mybir
+from concourse.masks import make_identity
+
+F32 = mybir.dt.float32
+BF16 = mybir.dt.bfloat16
+I32 = mybir.dt.int32
+U32 = mybir.dt.uint32
+U8 = mybir.dt.uint8
+FP8X4 = mybir.dt.float8_e4m3fn_x4
+FP4X4 = mybir.dt.float4_e2m1fn_x4
+ACT = mybir.ActivationFunctionType
+ALU = mybir.AluOpType
+
+P = 128
+BATCH = 8192
+IN = 1024
+H = 128
+GATES = 4 * H
+SIGMOID_COLS = 3 * H
+PACK = 4
+K_PASS = P * PACK
+PASSES = IN // K_PASS
+WORD_HALVES = 2
+
+ROW_TILES = BATCH // P
+TILES_PER_ROUND = 2
+ROUNDS = ROW_TILES // TILES_PER_ROUND
+ROUNDS_PER_CHUNK = 2
+TILES_PER_CHUNK = TILES_PER_ROUND * ROUNDS_PER_CHUNK
+CHUNKS = ROW_TILES // TILES_PER_CHUNK
+LOAD_AHEAD = 3
+X_AHEAD = 2
+PLAIN_AHEAD = 3
+STATE_AHEAD = 4
+
+FLOPS = 2 * BATCH * (IN + H) * GATES
+
+
+def tile_multiinputlstmcell_pa_t_kernel(
+    tc,
+    input_,
+    c_input,
+    h_0,
+    weight_ih_words,
+    weight_ih_scales,
+    weight_hh,
+    alpha_weight_ih_words,
+    alpha_weight_ih_scales,
+    alpha_weight_hh,
+    bias,
+    alpha_bias,
+    out_0,
+    out_1,
+):
+    nc = tc.nc
+    x_rows = input_.rearrange("(p t) k -> p t k", t=ROW_TILES)
+    h_rows = h_0.rearrange("(p t) h -> p t h", t=ROW_TILES)
+    c_rows = c_input.rearrange("(p t) o h -> p t (o h)", t=ROW_TILES)
+    h1_rows = out_0.rearrange("(p t) h -> p t h", t=ROW_TILES)
+    c1_rows = out_1.rearrange("(p t) h -> p t h", t=ROW_TILES)
+
+    with ExitStack() as ctx:
+        consts = ctx.enter_context(tc.tile_pool(name="consts", bufs=1))
+        loads = ctx.enter_context(tc.tile_pool(name="loads", bufs=LOAD_AHEAD + 1))
+        cells = ctx.enter_context(tc.tile_pool(name="cells", bufs=LOAD_AHEAD + 4))
+        rounds = ctx.enter_context(tc.tile_pool(name="rounds", bufs=3))
+        sums = ctx.enter_context(tc.tile_pool(name="sums", bufs=(PLAIN_AHEAD + 1) * TILES_PER_ROUND))
+        chunks = ctx.enter_context(tc.tile_pool(name="chunks", bufs=4))
+        psum = ctx.enter_context(tc.psum_pool(name="psum", bufs=2))
+        ctx.enter_context(tc.manual_schedule())
+
+        x_tiles = {}
+        h_tiles = {}
+        c_tiles = {}
+
+        def load(chunk):
+            if chunk >= CHUNKS:
+                return
+            rows = slice(chunk * TILES_PER_CHUNK, (chunk + 1) * TILES_PER_CHUNK)
+            h_sb = loads.tile([P, TILES_PER_CHUNK, H], BF16)
+            nc.sync.dma_start(out=h_sb[:], in_=h_rows[:, rows, :])
+            c_sb = cells.tile([P, TILES_PER_CHUNK, H], BF16)
+            nc.sync.dma_start(out=c_sb[:], in_=c_rows[:, rows, :])
+            x_sb = loads.tile([P, TILES_PER_CHUNK, IN], BF16)
+            nc.sync.dma_start(out=x_sb[:], in_=x_rows[:, rows, :])
+            x_tiles[chunk] = x_sb
+            h_tiles[chunk] = h_sb
+            c_tiles[chunk] = c_sb
+
+        load(0)
+
+        w4_words = consts.tile([P, PASSES, 2 * GATES], U8, align_bytes=64)
+        nc.sync.dma_start(
+            out=w4_words[:, :, 0 : 2 * H].bitcast(I32),
+            in_=alpha_weight_ih_words.rearrange("g p n -> p g n").bitcast(I32),
+        )
+        nc.sync.dma_start(
+            out=w4_words[:, :, 2 * H : 2 * GATES].bitcast(I32),
+            in_=weight_ih_words.rearrange("g p n -> p g n").bitcast(I32),
+        )
+        w4_scales = consts.tile([P, PASSES, GATES], U8, align_bytes=64)
+        nc.vector.memset(w4_scales[:].bitcast(I32), 0)
+        for quadrant in range(4):
+            live = slice(32 * quadrant, 32 * quadrant + 4)
+            given = slice(4 * quadrant, 4 * quadrant + 4)
+            nc.sync.dma_start(
+                out=w4_scales[live, :, 0:H].bitcast(I32),
+                in_=alpha_weight_ih_scales[:, given, :].rearrange("g r n -> r g n").bitcast(I32),
+            )
+            nc.sync.dma_start(
+                out=w4_scales[live, :, H:GATES].bitcast(I32),
+                in_=weight_ih_scales[:, given, :].rearrange("g r n -> r g n").bitcast(I32),
+            )
+        w_plain = consts.tile([P, GATES], BF16)
+        nc.scalar.dma_start(out=w_plain[:, 0:H], in_=alpha_weight_hh)
+        nc.scalar.dma_start(out=w_plain[:, H:GATES], in_=weight_hh)
+        bias_bf = consts.tile([P, GATES], BF16)
+        nc.scalar.dma_start(out=bias_bf[:, 0:H], in_=alpha_bias.partition_broadcast(P))
+        nc.scalar.dma_start(out=bias_bf[:, H:GATES], in_=bias.partition_broadcast(P))
+        bias_f32 = consts.tile([P, GATES], F32)
+        nc.vector.tensor_copy(out=bias_f32[:], in_=bias_bf[:])
+        ident_f32 = consts.tile([P, P], F32)
+        make_identity(nc, ident_f32[:])
+        ident_bf = consts.tile([P, P], BF16)
+        make_identity(nc, ident_bf[:])
+
+        for chunk in range(1, LOAD_AHEAD):
+            load(chunk)
+
+        state_t_tiles = {}
+        grouped_tiles = {}
+        code_tiles = {}
+        plain_tiles = {}
+        pre_tiles = {}
+        gate_tiles = {}
+        tail_tiles = {}
+
+        def transpose_state(chunk):
+            if not 0 <= chunk < CHUNKS:
+                return
+            state_ps = psum.tile([P, TILES_PER_CHUNK, 2, P], BF16)
+            for j in range(TILES_PER_CHUNK):
+                nc.tensor.transpose(state_ps[:, j, 0, :], h_tiles[chunk][:, j, :], ident_bf[:])
+                nc.tensor.transpose(state_ps[:, j, 1, :], c_tiles[chunk][:, j, :], ident_bf[:])
+            state_t = chunks.tile([P, TILES_PER_CHUNK, 2, P], BF16)
+            nc.scalar.copy(out=state_t[:], in_=state_ps[:])
+            state_t_tiles[chunk] = state_t
+
+        def transpose_x(rnd):
+            if not 0 <= rnd < ROUNDS:
+                return
+            chunk, half = divmod(rnd, ROUNDS_PER_CHUNK)
+            x_words = x_tiles[chunk][:].bitcast(F32)
+            grouped = rounds.tile([P, TILES_PER_ROUND, PASSES, P, PACK], BF16, align_bytes=64)
+            grouped_words = grouped[:].bitcast(F32)
+            for i in range(TILES_PER_ROUND):
+                j = half * TILES_PER_ROUND + i
+                x_ps = psum.tile([P, PASSES, WORD_HALVES, P], F32)
+                for g in range(PASSES):
+                    for u in range(WORD_HALVES):
+                        first = g * P * WORD_HALVES + u
+                        last = (g + 1) * P * WORD_HALVES
+                        nc.tensor.transpose(
+                            x_ps[:, g, u, :], x_words[:, j, first:last:WORD_HALVES], ident_f32[:]
+                        )
+                nc.scalar.copy(out=grouped_words[:, i], in_=x_ps[:].rearrange("p g u b -> p g b u"))
+            grouped_tiles[rnd] = grouped
+
+        def quantise(rnd):
+            if not 0 <= rnd < ROUNDS:
+                return
+            codes = rounds.tile([P, TILES_PER_ROUND, PASSES, P], U32, align_bytes=64)
+            scales = rounds.tile([P, TILES_PER_ROUND, PASSES, P], U8, align_bytes=64)
+            nc.vector.quantize_mx(
+                out=codes[:].rearrange("p i g b -> p (i g b)").bitcast(FP8X4),
+                scales=scales[:].rearrange("p i g b -> p (i g b)"),
+                in_=grouped_tiles[rnd][:].rearrange("p i g b t -> p (i g b t)"),
+            )
+            code_tiles[rnd] = (codes, scales)
+
+        def plain_products(rnd):
+            if not 0 <= rnd < ROUNDS:
+                return
+            chunk, half = divmod(rnd, ROUNDS_PER_CHUNK)
+            state_t = state_t_tiles[chunk]
+            for i in range(TILES_PER_ROUND):
+                j = half * TILES_PER_ROUND + i
+                plain_ps = psum.tile([P, GATES], F32)
+                nc.tensor.matmul(
+                    out=plain_ps[:, 0:H], lhsT=state_t[:, j, 1, :], rhs=w_plain[:, 0:H], start=True, stop=True
+                )
+                nc.tensor.matmul(
+                    out=plain_ps[:, H:GATES], lhsT=state_t[:, j, 0, :], rhs=w_plain[:, H:GATES], start=True, stop=True
+                )
+                plain_sb = sums.tile([P, GATES], F32)
+                nc.vector.tensor_tensor(out=plain_sb[:], in0=plain_ps[:], in1=bias_f32[:], op=ALU.add)
+                plain_tiles[rnd * TILES_PER_ROUND + i] = plain_sb
+
+        def mx_products(rnd):
+            if not 0 <= rnd < ROUNDS:
+                return
+            chunk, half = divmod(rnd, ROUNDS_PER_CHUNK)
+            if half == 0:
+                pre = chunks.tile([P, TILES_PER_CHUNK, GATES], F32)
+                pre_tiles[chunk] = pre
+            codes, scales = code_tiles[rnd]
+            for i in range(TILES_PER_ROUND):
+                j = half * TILES_PER_ROUND + i
+                mx_ps = psum.tile([P, GATES], F32)
+                for g in range(PASSES):
+                    nc.tensor.matmul_mx(
+                        out=mx_ps[:],
+                        lhsT=codes[:, i, g, :].bitcast(FP8X4),
+                        lhsT_scale=scales[:, i, g, :],
+                        rhs=w4_words[:, g, :].bitcast(FP4X4),
+                        rhs_scale=w4_scales[:, g, :],
+                        start=(g == 0),
+                        stop=(g == PASSES - 1),
+                    )
+                nc.vector.tensor_tensor(
+                    out=pre_tiles[chunk][:, j, :],
+                    in0=mx_ps[:],
+                    in1=plain_tiles[rnd * TILES_PER_ROUND + i][:],
+                    op=ALU.add,
+                )
+
+        def gates(rnd):
+            if not 0 <= rnd < ROUNDS:
+                return
+            chunk, half = divmod(rnd, ROUNDS_PER_CHUNK)
+            if half == 0:
+                gate = chunks.tile([P, TILES_PER_CHUNK, GATES], F32)
+                gate_tiles[chunk] = gate
+            rows = slice(half * TILES_PER_ROUND, (half + 1) * TILES_PER_ROUND)
+            pre = pre_tiles[chunk]
+            gate = gate_tiles[chunk]
+            nc.scalar.activation(
+                out=gate[:, rows, 0:SIGMOID_COLS], in_=pre[:, rows, 0:SIGMOID_COLS], func=ACT.Sigmoid
+            )
+            nc.scalar.activation(
+                out=gate[:, rows, SIGMOID_COLS:GATES], in_=pre[:, rows, SIGMOID_COLS:GATES], func=ACT.Tanh
+            )
+
+        def blend_inputs(chunk):
+            if not 0 <= chunk < CHUNKS:
+                return
+            gate = gate_tiles[chunk]
+            i_minus_a = chunks.tile([P, TILES_PER_CHUNK, H], F32)
+            nc.gpsimd.tensor_tensor(
+                out=i_minus_a[:], in0=gate[:, :, H : 2 * H], in1=gate[:, :, 0:H], op=ALU.subtract
+            )
+            g_minus_c = chunks.tile([P, TILES_PER_CHUNK, H], F32)
+            nc.gpsimd.tensor_tensor(
+                out=g_minus_c[:], in0=gate[:, :, 3 * H : 4 * H], in1=c_tiles[chunk][:], op=ALU.subtract
+            )
+            tail_tiles[("i_minus_a", chunk)] = i_minus_a
+            tail_tiles[("g_minus_c", chunk)] = g_minus_c
+
+        def blend(chunk):
+            if not 0 <= chunk < CHUNKS:
+                return
+            rows = slice(chunk * TILES_PER_CHUNK, (chunk + 1) * TILES_PER_CHUNK)
+            w_i = chunks.tile([P, TILES_PER_CHUNK, H], F32)
+            nc.scalar.activation(out=w_i[:], in_=tail_tiles[("i_minus_a", chunk)][:], func=ACT.Sigmoid)
+            step = chunks.tile([P, TILES_PER_CHUNK, H], F32)
+            nc.gpsimd.tensor_tensor(out=step[:], in0=w_i[:], in1=tail_tiles[("g_minus_c", chunk)][:], op=ALU.mult)
+            c_1 = chunks.tile([P, TILES_PER_CHUNK, H], F32)
+            nc.gpsimd.tensor_tensor(out=c_1[:], in0=step[:], in1=c_tiles[chunk][:], op=ALU.add)
+            nc.sync.dma_start(out=c1_rows[:, rows, :], in_=c_1[:])
+            tail_tiles[("c_1", chunk)] = c_1
+
+        def cell_tanh(chunk):
+            if not 0 <= chunk < CHUNKS:
+                return
+            tanh_c1 = chunks.tile([P, TILES_PER_CHUNK, H], F32)
+            nc.scalar.activation(out=tanh_c1[:], in_=tail_tiles[("c_1", chunk)][:], func=ACT.Tanh)
+            tail_tiles[("tanh_c1", chunk)] = tanh_c1
+
+        def hidden(chunk):
+            if not 0 <= chunk < CHUNKS:
+                return
+            rows = slice(chunk * TILES_PER_CHUNK, (chunk + 1) * TILES_PER_CHUNK)
+            h_1 = chunks.tile([P, TILES_PER_CHUNK, H], F32)
+            nc.vector.tensor_tensor(
+                out=h_1[:], in0=gate_tiles[chunk][:, :, 2 * H : 3 * H], in1=tail_tiles[("tanh_c1", chunk)][:], op=ALU.mult
+            )
+            nc.sync.dma_start(out=h1_rows[:, rows, :], in_=h_1[:])
+
+        for s in range(-STATE_AHEAD, ROUNDS + 4):
+            if s % ROUNDS_PER_CHUNK == 0 and s >= -X_AHEAD:
+                load((s + X_AHEAD) // ROUNDS_PER_CHUNK + LOAD_AHEAD)
+            transpose_x(s + X_AHEAD)
+            if s % ROUNDS_PER_CHUNK == 0:
+                transpose_state((s + STATE_AHEAD) // ROUNDS_PER_CHUNK)
+            quantise(s + 1)
+            plain_products(s + PLAIN_AHEAD)
+            mx_products(s)
+            gates(s - 1)
+            if s % ROUNDS_PER_CHUNK == 0:
+                blend_inputs((s - 2) // ROUNDS_PER_CHUNK)
+                cell_tanh((s - 4) // ROUNDS_PER_CHUNK)
+            else:
+                hidden((s - 5) // ROUNDS_PER_CHUNK)
+                blend((s - 3) // ROUNDS_PER_CHUNK)

@@ -248,7 +248,7 @@ def tile_multiinputlstmcell_pa_t_kernel(
                 return
             gate = gate_tiles[chunk]
             i_minus_a = chunks.tile([P, TILES_PER_CHUNK, H], F32)
-            nc.gpsimd.tensor_tensor(
+            nc.vector.tensor_tensor(
                 out=i_minus_a[:], in0=gate[:, :, H : 2 * H], in1=gate[:, :, 0:H], op=ALU.subtract
             )
             g_minus_c = chunks.tile([P, TILES_PER_CHUNK, H], F32)

@@ -25,15 +25,16 @@ PASSES = IN // K_PASS
 WORD_HALVES = 2
 
 ROW_TILES = BATCH // P
-TILES_PER_ROUND = 2
+TILES_PER_ROUND = 1
 ROUNDS = ROW_TILES // TILES_PER_ROUND
-ROUNDS_PER_CHUNK = 2
+ROUNDS_PER_CHUNK = 4
+HALF_CHUNK = ROUNDS_PER_CHUNK // 2
 TILES_PER_CHUNK = TILES_PER_ROUND * ROUNDS_PER_CHUNK
 CHUNKS = ROW_TILES // TILES_PER_CHUNK
 LOAD_AHEAD = 3
-X_AHEAD = 2
-PLAIN_AHEAD = 3
-STATE_AHEAD = 4
+X_AHEAD = 3
+PLAIN_AHEAD = 6
+STATE_AHEAD = 8
 
 FLOPS = 2 * BATCH * (IN + H) * GATES
 
@@ -65,7 +66,7 @@ def tile_multiinputlstmcell_pa_t_kernel(
         consts = ctx.enter_context(tc.tile_pool(name="consts", bufs=1))
         loads = ctx.enter_context(tc.tile_pool(name="loads", bufs=LOAD_AHEAD + 1))
         cells = ctx.enter_context(tc.tile_pool(name="cells", bufs=LOAD_AHEAD + 4))
-        rounds = ctx.enter_context(tc.tile_pool(name="rounds", bufs=3))
+        rounds = ctx.enter_context(tc.tile_pool(name="rounds", bufs=X_AHEAD + 1))
         sums = ctx.enter_context(tc.tile_pool(name="sums", bufs=(PLAIN_AHEAD + 1) * TILES_PER_ROUND))
         chunks = ctx.enter_context(tc.tile_pool(name="chunks", bufs=4))
         psum = ctx.enter_context(tc.psum_pool(name="psum", bufs=2))
@@ -248,7 +249,7 @@ def tile_multiinputlstmcell_pa_t_kernel(
                 return
             gate = gate_tiles[chunk]
             i_minus_a = chunks.tile([P, TILES_PER_CHUNK, H], F32)
-            nc.vector.tensor_tensor(
+            nc.gpsimd.tensor_tensor(
                 out=i_minus_a[:], in0=gate[:, :, H : 2 * H], in1=gate[:, :, 0:H], op=ALU.subtract
             )
             g_minus_c = chunks.tile([P, TILES_PER_CHUNK, H], F32)
@@ -288,19 +289,20 @@ def tile_multiinputlstmcell_pa_t_kernel(
             )
             nc.sync.dma_start(out=h1_rows[:, rows, :], in_=h_1[:])
 
-        for s in range(-STATE_AHEAD, ROUNDS + 4):
-            if s % ROUNDS_PER_CHUNK == 0 and s >= -X_AHEAD:
-                load((s + X_AHEAD) // ROUNDS_PER_CHUNK + LOAD_AHEAD)
+        for s in range(-STATE_AHEAD, ROUNDS + 3 * HALF_CHUNK + 1):
+            chunk, phase = divmod(s, ROUNDS_PER_CHUNK)
+            if phase == 0 and chunk >= 0:
+                load(chunk + LOAD_AHEAD)
             transpose_x(s + X_AHEAD)
-            if s % ROUNDS_PER_CHUNK == 0:
-                transpose_state((s + STATE_AHEAD) // ROUNDS_PER_CHUNK)
+            if phase == 0:
+                transpose_state(chunk + STATE_AHEAD // ROUNDS_PER_CHUNK)
             quantise(s + 1)
             plain_products(s + PLAIN_AHEAD)
             mx_products(s)
             gates(s - 1)
-            if s % ROUNDS_PER_CHUNK == 0:
-                blend_inputs((s - 2) // ROUNDS_PER_CHUNK)
-                cell_tanh((s - 4) // ROUNDS_PER_CHUNK)
-            else:
-                hidden((s - 5) // ROUNDS_PER_CHUNK)
-                blend((s - 3) // ROUNDS_PER_CHUNK)
+            if phase == 0:
+                blend_inputs(chunk - 1)
+                cell_tanh(chunk - 2)
+            if phase == HALF_CHUNK:
+                hidden(chunk - 2)
+                blend(chunk - 1)

@@ -25,16 +25,16 @@ PASSES = IN // K_PASS
 WORD_HALVES = 2
 
 ROW_TILES = BATCH // P
-TILES_PER_ROUND = 1
+TILES_PER_ROUND = 2
 ROUNDS = ROW_TILES // TILES_PER_ROUND
-ROUNDS_PER_CHUNK = 4
+ROUNDS_PER_CHUNK = 2
 HALF_CHUNK = ROUNDS_PER_CHUNK // 2
 TILES_PER_CHUNK = TILES_PER_ROUND * ROUNDS_PER_CHUNK
 CHUNKS = ROW_TILES // TILES_PER_CHUNK
 LOAD_AHEAD = 3
-X_AHEAD = 3
-PLAIN_AHEAD = 6
-STATE_AHEAD = 8
+X_AHEAD = 2
+PLAIN_AHEAD = 3
+STATE_AHEAD = 4
 
 FLOPS = 2 * BATCH * (IN + H) * GATES
 
@@ -249,7 +249,7 @@ def tile_multiinputlstmcell_pa_t_kernel(
                 return
             gate = gate_tiles[chunk]
             i_minus_a = chunks.tile([P, TILES_PER_CHUNK, H], F32)
-            nc.gpsimd.tensor_tensor(
+            nc.vector.tensor_tensor(
                 out=i_minus_a[:], in0=gate[:, :, H : 2 * H], in1=gate[:, :, 0:H], op=ALU.subtract
             )
             g_minus_c = chunks.tile([P, TILES_PER_CHUNK, H], F32)
@@ -289,7 +289,7 @@ def tile_multiinputlstmcell_pa_t_kernel(
             )
             nc.sync.dma_start(out=h1_rows[:, rows, :], in_=h_1[:])
 
-        for s in range(-STATE_AHEAD, ROUNDS + 3 * HALF_CHUNK + 1):
+        for s in range(-STATE_AHEAD, ROUNDS + 2 * ROUNDS_PER_CHUNK + 1):
             chunk, phase = divmod(s, ROUNDS_PER_CHUNK)
             if phase == 0 and chunk >= 0:
                 load(chunk + LOAD_AHEAD)
@@ -301,8 +301,8 @@ def tile_multiinputlstmcell_pa_t_kernel(
             mx_products(s)
             gates(s - 1)
             if phase == 0:
+                hidden(chunk - 3)
                 blend_inputs(chunk - 1)
-                cell_tanh(chunk - 2)
             if phase == HALF_CHUNK:
-                hidden(chunk - 2)
+                cell_tanh(chunk - 2)
                 blend(chunk - 1)

@@ -56,11 +56,11 @@ def tile_multiinputlstmcell_pa_t_kernel(
     out_1,
 ):
     nc = tc.nc
-    x_rows = input_.rearrange("(p t) k -> p t k", t=ROW_TILES)
-    h_rows = h_0.rearrange("(p t) h -> p t h", t=ROW_TILES)
-    c_rows = c_input.rearrange("(p t) o h -> p t (o h)", t=ROW_TILES)
-    h1_rows = out_0.rearrange("(p t) h -> p t h", t=ROW_TILES)
-    c1_rows = out_1.rearrange("(p t) h -> p t h", t=ROW_TILES)
+    x_rows = input_.rearrange("(c p j) k -> c p j k", p=P, j=TILES_PER_CHUNK)
+    h_rows = h_0.rearrange("(c p j) h -> c p j h", p=P, j=TILES_PER_CHUNK)
+    c_rows = c_input.rearrange("(c p j) o h -> c p j (o h)", p=P, j=TILES_PER_CHUNK)
+    h1_rows = out_0.rearrange("(c p j) h -> c p j h", p=P, j=TILES_PER_CHUNK)
+    c1_rows = out_1.rearrange("(c p j) h -> c p j h", p=P, j=TILES_PER_CHUNK)
 
     with ExitStack() as ctx:
         consts = ctx.enter_context(tc.tile_pool(name="consts", bufs=1))
@@ -79,13 +79,12 @@ def tile_multiinputlstmcell_pa_t_kernel(
         def load(chunk):
             if chunk >= CHUNKS:
                 return
-            rows = slice(chunk * TILES_PER_CHUNK, (chunk + 1) * TILES_PER_CHUNK)
             h_sb = loads.tile([P, TILES_PER_CHUNK, H], BF16)
-            nc.sync.dma_start(out=h_sb[:], in_=h_rows[:, rows, :])
+            nc.sync.dma_start(out=h_sb[:], in_=h_rows[chunk])
             c_sb = cells.tile([P, TILES_PER_CHUNK, H], BF16)
-            nc.sync.dma_start(out=c_sb[:], in_=c_rows[:, rows, :])
+            nc.sync.dma_start(out=c_sb[:], in_=c_rows[chunk])
             x_sb = loads.tile([P, TILES_PER_CHUNK, IN], BF16)
-            nc.sync.dma_start(out=x_sb[:], in_=x_rows[:, rows, :])
+            nc.sync.dma_start(out=x_sb[:], in_=x_rows[chunk])
             x_tiles[chunk] = x_sb
             h_tiles[chunk] = h_sb
             c_tiles[chunk] = c_sb
@@ -262,14 +261,13 @@ def tile_multiinputlstmcell_pa_t_kernel(
         def blend(chunk):
             if not 0 <= chunk < CHUNKS:
                 return
-            rows = slice(chunk * TILES_PER_CHUNK, (chunk + 1) * TILES_PER_CHUNK)
             w_i = chunks.tile([P, TILES_PER_CHUNK, H], F32)
             nc.scalar.activation(out=w_i[:], in_=tail_tiles[("i_minus_a", chunk)][:], func=ACT.Sigmoid)
             step = chunks.tile([P, TILES_PER_CHUNK, H], F32)
             nc.gpsimd.tensor_tensor(out=step[:], in0=w_i[:], in1=tail_tiles[("g_minus_c", chunk)][:], op=ALU.mult)
             c_1 = chunks.tile([P, TILES_PER_CHUNK, H], F32)
             nc.gpsimd.tensor_tensor(out=c_1[:], in0=step[:], in1=c_tiles[chunk][:], op=ALU.add)
-            nc.sync.dma_start(out=c1_rows[:, rows, :], in_=c_1[:])
+            nc.sync.dma_start(out=c1_rows[chunk], in_=c_1[:])
             tail_tiles[("c_1", chunk)] = c_1
 
         def cell_tanh(chunk):
@@ -282,12 +280,11 @@ def tile_multiinputlstmcell_pa_t_kernel(
         def hidden(chunk):
             if not 0 <= chunk < CHUNKS:
                 return
-            rows = slice(chunk * TILES_PER_CHUNK, (chunk + 1) * TILES_PER_CHUNK)
             h_1 = chunks.tile([P, TILES_PER_CHUNK, H], F32)
             nc.vector.tensor_tensor(
                 out=h_1[:], in0=gate_tiles[chunk][:, :, 2 * H : 3 * H], in1=tail_tiles[("tanh_c1", chunk)][:], op=ALU.mult
             )
-            nc.sync.dma_start(out=h1_rows[:, rows, :], in_=h_1[:])
+            nc.sync.dma_start(out=h1_rows[chunk], in_=h_1[:])
 
         for s in range(-STATE_AHEAD, ROUNDS + 2 * ROUNDS_PER_CHUNK + 1):
             chunk, phase = divmod(s, ROUNDS_PER_CHUNK)

@@ -248,7 +248,7 @@ def tile_multiinputlstmcell_pa_t_kernel(
                 return
             gate = gate_tiles[chunk]
             i_minus_a = chunks.tile([P, TILES_PER_CHUNK, H], F32)
-            nc.vector.tensor_tensor(
+            nc.gpsimd.tensor_tensor(
                 out=i_minus_a[:], in0=gate[:, :, H : 2 * H], in1=gate[:, :, 0:H], op=ALU.subtract
             )
             g_minus_c = chunks.tile([P, TILES_PER_CHUNK, H], F32)

@@ -34,6 +34,7 @@ CHUNKS = ROW_TILES // TILES_PER_CHUNK
 LOAD_AHEAD = 3
 X_AHEAD = 2
 PLAIN_AHEAD = 3
+CHUNKS_ENDING_ON_VECTOR = 2
 STATE_AHEAD = 4
 
 FLOPS = 2 * BATCH * (IN + H) * GATES
@@ -243,16 +244,19 @@ def tile_multiinputlstmcell_pa_t_kernel(
                 out=gate[:, rows, SIGMOID_COLS:GATES], in_=pre[:, rows, SIGMOID_COLS:GATES], func=ACT.Tanh
             )
 
+        def tail_engine(chunk):
+            return nc.vector if chunk >= CHUNKS - CHUNKS_ENDING_ON_VECTOR else nc.gpsimd
+
         def blend_inputs(chunk):
             if not 0 <= chunk < CHUNKS:
                 return
             gate = gate_tiles[chunk]
             i_minus_a = chunks.tile([P, TILES_PER_CHUNK, H], F32)
-            nc.gpsimd.tensor_tensor(
+            tail_engine(chunk).tensor_tensor(
                 out=i_minus_a[:], in0=gate[:, :, H : 2 * H], in1=gate[:, :, 0:H], op=ALU.subtract
             )
             g_minus_c = chunks.tile([P, TILES_PER_CHUNK, H], F32)
-            nc.gpsimd.tensor_tensor(
+            tail_engine(chunk).tensor_tensor(
                 out=g_minus_c[:], in0=gate[:, :, 3 * H : 4 * H], in1=c_tiles[chunk][:], op=ALU.subtract
             )
             tail_tiles[("i_minus_a", chunk)] = i_minus_a
@@ -264,9 +268,9 @@ def tile_multiinputlstmcell_pa_t_kernel(
             w_i = chunks.tile([P, TILES_PER_CHUNK, H], F32)
             nc.scalar.activation(out=w_i[:], in_=tail_tiles[("i_minus_a", chunk)][:], func=ACT.Sigmoid)
             step = chunks.tile([P, TILES_PER_CHUNK, H], F32)
-            nc.gpsimd.tensor_tensor(out=step[:], in0=w_i[:], in1=tail_tiles[("g_minus_c", chunk)][:], op=ALU.mult)
+            tail_engine(chunk).tensor_tensor(out=step[:], in0=w_i[:], in1=tail_tiles[("g_minus_c", chunk)][:], op=ALU.mult)
             c_1 = chunks.tile([P, TILES_PER_CHUNK, H], F32)
-            nc.gpsimd.tensor_tensor(out=c_1[:], in0=step[:], in1=c_tiles[chunk][:], op=ALU.add)
+            tail_engine(chunk).tensor_tensor(out=c_1[:], in0=step[:], in1=c_tiles[chunk][:], op=ALU.add)
             nc.sync.dma_start(out=c1_rows[chunk], in_=c_1[:])
             tail_tiles[("c_1", chunk)] = c_1
 

@@ -32,6 +32,7 @@ HALF_CHUNK = ROUNDS_PER_CHUNK // 2
 TILES_PER_CHUNK = TILES_PER_ROUND * ROUNDS_PER_CHUNK
 CHUNKS = ROW_TILES // TILES_PER_CHUNK
 LOAD_AHEAD = 3
+STATE_LOAD_AHEAD = 4
 X_AHEAD = 2
 PLAIN_AHEAD = 3
 CHUNKS_ENDING_ON_VECTOR = 2
@@ -66,7 +67,8 @@ def tile_multiinputlstmcell_pa_t_kernel(
     with ExitStack() as ctx:
         consts = ctx.enter_context(tc.tile_pool(name="consts", bufs=1))
         loads = ctx.enter_context(tc.tile_pool(name="loads", bufs=LOAD_AHEAD + 1))
-        cells = ctx.enter_context(tc.tile_pool(name="cells", bufs=LOAD_AHEAD + 4))
+        hiddens = ctx.enter_context(tc.tile_pool(name="hiddens", bufs=STATE_LOAD_AHEAD + 1))
+        cells = ctx.enter_context(tc.tile_pool(name="cells", bufs=STATE_LOAD_AHEAD + 4))
         rounds = ctx.enter_context(tc.tile_pool(name="rounds", bufs=X_AHEAD + 1))
         sums = ctx.enter_context(tc.tile_pool(name="sums", bufs=(PLAIN_AHEAD + 1) * TILES_PER_ROUND))
         chunks = ctx.enter_context(tc.tile_pool(name="chunks", bufs=4))
@@ -77,20 +79,25 @@ def tile_multiinputlstmcell_pa_t_kernel(
         h_tiles = {}
         c_tiles = {}
 
-        def load(chunk):
+        def load_state(chunk):
             if chunk >= CHUNKS:
                 return
-            h_sb = loads.tile([P, TILES_PER_CHUNK, H], BF16)
+            h_sb = hiddens.tile([P, TILES_PER_CHUNK, H], BF16)
             nc.sync.dma_start(out=h_sb[:], in_=h_rows[chunk])
             c_sb = cells.tile([P, TILES_PER_CHUNK, H], BF16)
             nc.sync.dma_start(out=c_sb[:], in_=c_rows[chunk])
-            x_sb = loads.tile([P, TILES_PER_CHUNK, IN], BF16)
-            nc.sync.dma_start(out=x_sb[:], in_=x_rows[chunk])
-            x_tiles[chunk] = x_sb
             h_tiles[chunk] = h_sb
             c_tiles[chunk] = c_sb
 
-        load(0)
+        def load_x(chunk):
+            if chunk >= CHUNKS:
+                return
+            x_sb = loads.tile([P, TILES_PER_CHUNK, IN], BF16)
+            nc.sync.dma_start(out=x_sb[:], in_=x_rows[chunk])
+            x_tiles[chunk] = x_sb
+
+        load_state(0)
+        load_x(0)
 
         w4_words = consts.tile([P, PASSES, 2 * GATES], U8, align_bytes=64)
         nc.sync.dma_start(
@@ -128,7 +135,10 @@ def tile_multiinputlstmcell_pa_t_kernel(
         make_identity(nc, ident_bf[:])
 
         for chunk in range(1, LOAD_AHEAD):
-            load(chunk)
+            load_state(chunk)
+            load_x(chunk)
+        for chunk in range(LOAD_AHEAD, STATE_LOAD_AHEAD):
+            load_state(chunk)
 
         state_t_tiles = {}
         grouped_tiles = {}
@@ -293,7 +303,8 @@ def tile_multiinputlstmcell_pa_t_kernel(
         for s in range(-STATE_AHEAD, ROUNDS + 2 * ROUNDS_PER_CHUNK + 1):
             chunk, phase = divmod(s, ROUNDS_PER_CHUNK)
             if phase == 0 and chunk >= 0:
-                load(chunk + LOAD_AHEAD)
+                load_state(chunk + STATE_LOAD_AHEAD)
+                load_x(chunk + LOAD_AHEAD)
             transpose_x(s + X_AHEAD)
             if phase == 0:
                 transpose_state(chunk + STATE_AHEAD // ROUNDS_PER_CHUNK)

@@ -96,6 +96,13 @@ def tile_multiinputlstmcell_pa_t_kernel(
             nc.sync.dma_start(out=x_sb[:], in_=x_rows[chunk])
             x_tiles[chunk] = x_sb
 
+        bias_row = consts.tile([P, GATES], BF16)
+        nc.vector.memset(bias_row[:], 0.0)
+        nc.sync.dma_start(out=bias_row[0:1, 0:H], in_=alpha_bias.unsqueeze(0))
+        nc.sync.dma_start(out=bias_row[0:1, H:GATES], in_=bias.unsqueeze(0))
+        ones_bf = consts.tile([P, P], BF16)
+        nc.vector.memset(ones_bf[:], 1.0)
+
         load_state(0)
         load_x(0)
 
@@ -124,11 +131,10 @@ def tile_multiinputlstmcell_pa_t_kernel(
         w_plain = consts.tile([P, GATES], BF16)
         nc.scalar.dma_start(out=w_plain[:, 0:H], in_=alpha_weight_hh)
         nc.scalar.dma_start(out=w_plain[:, H:GATES], in_=weight_hh)
-        bias_bf = consts.tile([P, GATES], BF16)
-        nc.scalar.dma_start(out=bias_bf[:, 0:H], in_=alpha_bias.partition_broadcast(P))
-        nc.scalar.dma_start(out=bias_bf[:, H:GATES], in_=bias.partition_broadcast(P))
         bias_f32 = consts.tile([P, GATES], F32)
-        nc.vector.tensor_copy(out=bias_f32[:], in_=bias_bf[:])
+        warm = consts.tile([P, 2], F32)
+        nc.vector.memset(warm[:], 0.0)
+        nc.scalar.activation(out=warm[:, 1:2], in_=warm[:, 0:1], func=ACT.Sigmoid)
         ident_f32 = consts.tile([P, P], F32)
         make_identity(nc, ident_f32[:])
         ident_bf = consts.tile([P, P], BF16)
@@ -158,6 +164,11 @@ def tile_multiinputlstmcell_pa_t_kernel(
             state_t = chunks.tile([P, TILES_PER_CHUNK, 2, P], BF16)
             nc.scalar.copy(out=state_t[:], in_=state_ps[:])
             state_t_tiles[chunk] = state_t
+
+        def spread_biases():
+            plain_ps = psum.tile([P, GATES], F32)
+            nc.tensor.matmul(out=plain_ps[:], lhsT=ones_bf[:], rhs=bias_row[:], start=True, stop=True)
+            nc.vector.tensor_copy(out=bias_f32[:], in_=plain_ps[:])
 
         def transpose_x(rnd):
             if not 0 <= rnd < ROUNDS:
@@ -308,6 +319,8 @@ def tile_multiinputlstmcell_pa_t_kernel(
             transpose_x(s + X_AHEAD)
             if phase == 0:
                 transpose_state(chunk + STATE_AHEAD // ROUNDS_PER_CHUNK)
+            if s == -STATE_AHEAD:
+                spread_biases()
             quantise(s + 1)
             plain_products(s + PLAIN_AHEAD)
             mx_products(s)

@@ -32,6 +32,7 @@ HALF_CHUNK = ROUNDS_PER_CHUNK // 2
 TILES_PER_CHUNK = TILES_PER_ROUND * ROUNDS_PER_CHUNK
 CHUNKS = ROW_TILES // TILES_PER_CHUNK
 LOAD_AHEAD = 3
+FIRST_LOADS = 2
 STATE_LOAD_AHEAD = 4
 X_AHEAD = 2
 PLAIN_AHEAD = 3
@@ -98,13 +99,15 @@ def tile_multiinputlstmcell_pa_t_kernel(
 
         bias_row = consts.tile([P, GATES], BF16)
         nc.vector.memset(bias_row[:], 0.0)
-        nc.sync.dma_start(out=bias_row[0:1, 0:H], in_=alpha_bias.unsqueeze(0))
-        nc.sync.dma_start(out=bias_row[0:1, H:GATES], in_=bias.unsqueeze(0))
         ones_bf = consts.tile([P, P], BF16)
         nc.vector.memset(ones_bf[:], 1.0)
 
-        load_state(0)
-        load_x(0)
+        for chunk in range(FIRST_LOADS):
+            load_state(chunk)
+            if chunk == 0:
+                nc.sync.dma_start(out=bias_row[0:1, 0:H], in_=alpha_bias.unsqueeze(0))
+                nc.sync.dma_start(out=bias_row[0:1, H:GATES], in_=bias.unsqueeze(0))
+            load_x(chunk)
 
         w4_words = consts.tile([P, PASSES, 2 * GATES], U8, align_bytes=64)
         nc.sync.dma_start(
@@ -140,7 +143,7 @@ def tile_multiinputlstmcell_pa_t_kernel(
         ident_bf = consts.tile([P, P], BF16)
         make_identity(nc, ident_bf[:])
 
-        for chunk in range(1, LOAD_AHEAD):
+        for chunk in range(FIRST_LOADS, LOAD_AHEAD):
             load_state(chunk)
             load_x(chunk)
         for chunk in range(LOAD_AHEAD, STATE_LOAD_AHEAD):

@@ -205,12 +205,12 @@ def tile_multiinputlstmcell_pa_t_kernel(
             )
             code_tiles[rnd] = (codes, scales)
 
-        def plain_products(rnd):
+        def plain_products(rnd, i):
             if not 0 <= rnd < ROUNDS:
                 return
             chunk, half = divmod(rnd, ROUNDS_PER_CHUNK)
             state_t = state_t_tiles[chunk]
-            for i in range(TILES_PER_ROUND):
+            if True:
                 j = half * TILES_PER_ROUND + i
                 plain_ps = psum.tile([P, GATES], F32)
                 nc.tensor.matmul(
@@ -325,8 +325,9 @@ def tile_multiinputlstmcell_pa_t_kernel(
             if s == -STATE_AHEAD:
                 spread_biases()
             quantise(s + 1)
-            plain_products(s + PLAIN_AHEAD)
+            plain_products(s + PLAIN_AHEAD, 0)
             mx_products(s)
+            plain_products(s + PLAIN_AHEAD, 1)
             gates(s - 1)
             if phase == 0:
                 hidden(chunk - 3)

@@ -28,16 +28,15 @@ ROW_TILES = BATCH // P
 TILES_PER_ROUND = 2
 ROUNDS = ROW_TILES // TILES_PER_ROUND
 ROUNDS_PER_CHUNK = 2
-HALF_CHUNK = ROUNDS_PER_CHUNK // 2
 TILES_PER_CHUNK = TILES_PER_ROUND * ROUNDS_PER_CHUNK
 CHUNKS = ROW_TILES // TILES_PER_CHUNK
 LOAD_AHEAD = 3
-FIRST_LOADS = 2
 STATE_LOAD_AHEAD = 4
 X_AHEAD = 2
-PLAIN_AHEAD = 3
-CHUNKS_ENDING_ON_VECTOR = 2
+PLAIN_AHEAD = 2
 STATE_AHEAD = 4
+CHUNKS_ENDING_ON_VECTOR = 2
+FIRST_ON_VECTOR = CHUNKS - CHUNKS_ENDING_ON_VECTOR
 
 FLOPS = 2 * BATCH * (IN + H) * GATES
 
@@ -90,11 +89,14 @@ def tile_multiinputlstmcell_pa_t_kernel(
             h_tiles[chunk] = h_sb
             c_tiles[chunk] = c_sb
 
-        def load_x(chunk):
+        def load_x(chunk, pieces=1):
             if chunk >= CHUNKS:
                 return
             x_sb = loads.tile([P, TILES_PER_CHUNK, IN], BF16)
-            nc.sync.dma_start(out=x_sb[:], in_=x_rows[chunk])
+            size = TILES_PER_CHUNK // pieces
+            for piece in range(pieces):
+                rows = slice(piece * size, (piece + 1) * size)
+                nc.sync.dma_start(out=x_sb[:, rows, :], in_=x_rows[chunk][:, rows, :])
             x_tiles[chunk] = x_sb
 
         bias_row = consts.tile([P, GATES], BF16)
@@ -102,12 +104,12 @@ def tile_multiinputlstmcell_pa_t_kernel(
         ones_bf = consts.tile([P, P], BF16)
         nc.vector.memset(ones_bf[:], 1.0)
 
-        for chunk in range(FIRST_LOADS):
-            load_state(chunk)
-            if chunk == 0:
-                nc.sync.dma_start(out=bias_row[0:1, 0:H], in_=alpha_bias.unsqueeze(0))
-                nc.sync.dma_start(out=bias_row[0:1, H:GATES], in_=bias.unsqueeze(0))
-            load_x(chunk)
+        load_state(0)
+        nc.sync.dma_start(out=bias_row[0:1, 0:H], in_=alpha_bias.unsqueeze(0))
+        nc.sync.dma_start(out=bias_row[0:1, H:GATES], in_=bias.unsqueeze(0))
+        load_x(0, pieces=ROUNDS_PER_CHUNK)
+        load_state(1)
+        load_x(1)
 
         w4_words = consts.tile([P, PASSES, 2 * GATES], U8, align_bytes=64)
         nc.sync.dma_start(
@@ -143,12 +145,11 @@ def tile_multiinputlstmcell_pa_t_kernel(
         ident_bf = consts.tile([P, P], BF16)
         make_identity(nc, ident_bf[:])
 
-        for chunk in range(FIRST_LOADS, LOAD_AHEAD):
-            load_state(chunk)
-            load_x(chunk)
-        for chunk in range(LOAD_AHEAD, STATE_LOAD_AHEAD):
-            load_state(chunk)
+        load_state(2)
+        load_x(2)
+        load_state(3)
 
+        state_banks = {}
         state_t_tiles = {}
         grouped_tiles = {}
         code_tiles = {}
@@ -157,16 +158,21 @@ def tile_multiinputlstmcell_pa_t_kernel(
         gate_tiles = {}
         tail_tiles = {}
 
-        def transpose_state(chunk):
-            if not 0 <= chunk < CHUNKS:
+        def transpose_state(rnd):
+            if not 0 <= rnd < ROUNDS:
                 return
-            state_ps = psum.tile([P, TILES_PER_CHUNK, 2, P], BF16)
-            for j in range(TILES_PER_CHUNK):
+            chunk, half = divmod(rnd, ROUNDS_PER_CHUNK)
+            if half == 0:
+                state_ps = psum.tile([P, TILES_PER_CHUNK, 2, P], BF16)
+                state_banks[chunk] = state_ps
+            state_ps = state_banks[chunk]
+            for j in range(half * TILES_PER_ROUND, (half + 1) * TILES_PER_ROUND):
                 nc.tensor.transpose(state_ps[:, j, 0, :], h_tiles[chunk][:, j, :], ident_bf[:])
                 nc.tensor.transpose(state_ps[:, j, 1, :], c_tiles[chunk][:, j, :], ident_bf[:])
-            state_t = chunks.tile([P, TILES_PER_CHUNK, 2, P], BF16)
-            nc.scalar.copy(out=state_t[:], in_=state_ps[:])
-            state_t_tiles[chunk] = state_t
+            if half == ROUNDS_PER_CHUNK - 1:
+                state_t = chunks.tile([P, TILES_PER_CHUNK, 2, P], BF16)
+                nc.scalar.copy(out=state_t[:], in_=state_ps[:])
+                state_t_tiles[chunk] = state_t
 
         def spread_biases():
             plain_ps = psum.tile([P, GATES], F32)
@@ -210,18 +216,17 @@ def tile_multiinputlstmcell_pa_t_kernel(
                 return
             chunk, half = divmod(rnd, ROUNDS_PER_CHUNK)
             state_t = state_t_tiles[chunk]
-            if True:
-                j = half * TILES_PER_ROUND + i
-                plain_ps = psum.tile([P, GATES], F32)
-                nc.tensor.matmul(
-                    out=plain_ps[:, 0:H], lhsT=state_t[:, j, 1, :], rhs=w_plain[:, 0:H], start=True, stop=True
-                )
-                nc.tensor.matmul(
-                    out=plain_ps[:, H:GATES], lhsT=state_t[:, j, 0, :], rhs=w_plain[:, H:GATES], start=True, stop=True
-                )
-                plain_sb = sums.tile([P, GATES], F32)
-                nc.vector.tensor_tensor(out=plain_sb[:], in0=plain_ps[:], in1=bias_f32[:], op=ALU.add)
-                plain_tiles[rnd * TILES_PER_ROUND + i] = plain_sb
+            j = half * TILES_PER_ROUND + i
+            plain_ps = psum.tile([P, GATES], F32)
+            nc.tensor.matmul(
+                out=plain_ps[:, 0:H], lhsT=state_t[:, j, 1, :], rhs=w_plain[:, 0:H], start=True, stop=True
+            )
+            nc.tensor.matmul(
+                out=plain_ps[:, H:GATES], lhsT=state_t[:, j, 0, :], rhs=w_plain[:, H:GATES], start=True, stop=True
+            )
+            plain_sb = sums.tile([P, GATES], F32)
+            nc.vector.tensor_tensor(out=plain_sb[:], in0=plain_ps[:], in1=bias_f32[:], op=ALU.add)
+            plain_tiles[rnd * TILES_PER_ROUND + i] = plain_sb
 
         def mx_products(rnd):
             if not 0 <= rnd < ROUNDS:
@@ -268,70 +273,89 @@ def tile_multiinputlstmcell_pa_t_kernel(
                 out=gate[:, rows, SIGMOID_COLS:GATES], in_=pre[:, rows, SIGMOID_COLS:GATES], func=ACT.Tanh
             )
 
-        def tail_engine(chunk):
-            return nc.vector if chunk >= CHUNKS - CHUNKS_ENDING_ON_VECTOR else nc.gpsimd
+        def tail_tile(name, chunk):
+            if (name, chunk) not in tail_tiles:
+                tail = chunks.tile([P, TILES_PER_CHUNK, H], F32, name=name)
+                tail_tiles[(name, chunk)] = tail
+            return tail_tiles[(name, chunk)]
 
-        def blend_inputs(chunk):
-            if not 0 <= chunk < CHUNKS:
-                return
+        def blend_inputs(chunk, rows, engine):
             gate = gate_tiles[chunk]
-            i_minus_a = chunks.tile([P, TILES_PER_CHUNK, H], F32)
-            tail_engine(chunk).tensor_tensor(
-                out=i_minus_a[:], in0=gate[:, :, H : 2 * H], in1=gate[:, :, 0:H], op=ALU.subtract
+            i_minus_a = tail_tile("i_minus_a", chunk)
+            engine.tensor_tensor(
+                out=i_minus_a[:, rows, :], in0=gate[:, rows, H : 2 * H], in1=gate[:, rows, 0:H], op=ALU.subtract
             )
-            g_minus_c = chunks.tile([P, TILES_PER_CHUNK, H], F32)
-            tail_engine(chunk).tensor_tensor(
-                out=g_minus_c[:], in0=gate[:, :, 3 * H : 4 * H], in1=c_tiles[chunk][:], op=ALU.subtract
+            g_minus_c = tail_tile("g_minus_c", chunk)
+            engine.tensor_tensor(
+                out=g_minus_c[:, rows, :], in0=gate[:, rows, 3 * H : 4 * H], in1=c_tiles[chunk][:, rows, :], op=ALU.subtract
             )
-            tail_tiles[("i_minus_a", chunk)] = i_minus_a
-            tail_tiles[("g_minus_c", chunk)] = g_minus_c
 
-        def blend(chunk):
-            if not 0 <= chunk < CHUNKS:
-                return
-            w_i = chunks.tile([P, TILES_PER_CHUNK, H], F32)
-            nc.scalar.activation(out=w_i[:], in_=tail_tiles[("i_minus_a", chunk)][:], func=ACT.Sigmoid)
-            step = chunks.tile([P, TILES_PER_CHUNK, H], F32)
-            tail_engine(chunk).tensor_tensor(out=step[:], in0=w_i[:], in1=tail_tiles[("g_minus_c", chunk)][:], op=ALU.mult)
-            c_1 = chunks.tile([P, TILES_PER_CHUNK, H], F32)
-            tail_engine(chunk).tensor_tensor(out=c_1[:], in0=step[:], in1=c_tiles[chunk][:], op=ALU.add)
-            nc.sync.dma_start(out=c1_rows[chunk], in_=c_1[:])
-            tail_tiles[("c_1", chunk)] = c_1
+        def pair_weight(chunk, rows):
+            w_i = tail_tile("w_i", chunk)
+            nc.scalar.activation(out=w_i[:, rows, :], in_=tail_tile("i_minus_a", chunk)[:, rows, :], func=ACT.Sigmoid)
 
-        def cell_tanh(chunk):
-            if not 0 <= chunk < CHUNKS:
-                return
-            tanh_c1 = chunks.tile([P, TILES_PER_CHUNK, H], F32)
-            nc.scalar.activation(out=tanh_c1[:], in_=tail_tiles[("c_1", chunk)][:], func=ACT.Tanh)
-            tail_tiles[("tanh_c1", chunk)] = tanh_c1
+        def blend(chunk, rows, engine):
+            step = tail_tile("step", chunk)
+            engine.tensor_tensor(
+                out=step[:, rows, :], in0=tail_tile("w_i", chunk)[:, rows, :], in1=tail_tile("g_minus_c", chunk)[:, rows, :], op=ALU.mult
+            )
+            c_1 = tail_tile("c_1", chunk)
+            engine.tensor_tensor(out=c_1[:, rows, :], in0=step[:, rows, :], in1=c_tiles[chunk][:, rows, :], op=ALU.add)
+            nc.sync.dma_start(out=c1_rows[chunk][:, rows, :], in_=c_1[:, rows, :])
 
-        def hidden(chunk):
-            if not 0 <= chunk < CHUNKS:
-                return
-            h_1 = chunks.tile([P, TILES_PER_CHUNK, H], F32)
+        def cell_tanh(chunk, rows):
+            tanh_c1 = tail_tile("tanh_c1", chunk)
+            nc.scalar.activation(out=tanh_c1[:, rows, :], in_=tail_tile("c_1", chunk)[:, rows, :], func=ACT.Tanh)
+
+        def hidden(chunk, rows):
+            h_1 = tail_tile("h_1", chunk)
             nc.vector.tensor_tensor(
-                out=h_1[:], in0=gate_tiles[chunk][:, :, 2 * H : 3 * H], in1=tail_tiles[("tanh_c1", chunk)][:], op=ALU.mult
+                out=h_1[:, rows, :],
+                in0=gate_tiles[chunk][:, rows, 2 * H : 3 * H],
+                in1=tail_tile("tanh_c1", chunk)[:, rows, :],
+                op=ALU.mult,
             )
-            nc.sync.dma_start(out=h1_rows[chunk], in_=h_1[:])
+            nc.sync.dma_start(out=h1_rows[chunk][:, rows, :], in_=h_1[:, rows, :])
+
+        def whole(chunk):
+            return [(chunk, slice(0, TILES_PER_CHUNK))] if 0 <= chunk < FIRST_ON_VECTOR else []
+
+        def part(rnd):
+            chunk, half = divmod(rnd, ROUNDS_PER_CHUNK)
+            rows = slice(half * TILES_PER_ROUND, (half + 1) * TILES_PER_ROUND)
+            return [(chunk, rows)] if FIRST_ON_VECTOR <= chunk < CHUNKS else []
 
         for s in range(-STATE_AHEAD, ROUNDS + 2 * ROUNDS_PER_CHUNK + 1):
             chunk, phase = divmod(s, ROUNDS_PER_CHUNK)
             if phase == 0 and chunk >= 0:
                 load_state(chunk + STATE_LOAD_AHEAD)
                 load_x(chunk + LOAD_AHEAD)
-            transpose_x(s + X_AHEAD)
-            if phase == 0:
-                transpose_state(chunk + STATE_AHEAD // ROUNDS_PER_CHUNK)
-            if s == -STATE_AHEAD:
-                spread_biases()
+            if phase == 1:
+                for where in whole(chunk - 1):
+                    pair_weight(*where)
+                    blend(*where, nc.gpsimd)
+            gates(s - 1)
             quantise(s + 1)
+            transpose_x(s + X_AHEAD)
             plain_products(s + PLAIN_AHEAD, 0)
             mx_products(s)
             plain_products(s + PLAIN_AHEAD, 1)
-            gates(s - 1)
+            transpose_state(s + STATE_AHEAD)
+            if s == -STATE_AHEAD:
+                spread_biases()
             if phase == 0:
-                hidden(chunk - 3)
-                blend_inputs(chunk - 1)
-            if phase == HALF_CHUNK:
-                cell_tanh(chunk - 2)
-                blend(chunk - 1)
+                for where in whole(chunk - 3):
+                    hidden(*where)
+                for where in whole(chunk - 1):
+                    blend_inputs(*where, nc.gpsimd)
+                for where in whole(chunk - 2):
+                    cell_tanh(*where)
+            for where in part(s - 1):
+                blend_inputs(*where, nc.vector)
+                pair_weight(*where)
+            for where in part(s - 2):
+                blend(*where, nc.vector)
+            for where in part(s - 3):
+                cell_tanh(*where)
+            for where in part(s - 4):
+                hidden(*where)

@@ -37,6 +37,7 @@ PLAIN_AHEAD = 2
 STATE_AHEAD = 4
 CHUNKS_ENDING_ON_VECTOR = 2
 FIRST_ON_VECTOR = CHUNKS - CHUNKS_ENDING_ON_VECTOR
+TILE_ON_SCALAR = TILES_PER_CHUNK - 1
 
 FLOPS = 2 * BATCH * (IN + H) * GATES
 
@@ -217,15 +218,25 @@ def tile_multiinputlstmcell_pa_t_kernel(
             chunk, half = divmod(rnd, ROUNDS_PER_CHUNK)
             state_t = state_t_tiles[chunk]
             j = half * TILES_PER_ROUND + i
+            scalar_empties = j == TILE_ON_SCALAR
             plain_ps = psum.tile([P, GATES], F32)
-            nc.tensor.matmul(
-                out=plain_ps[:, 0:H], lhsT=state_t[:, j, 1, :], rhs=w_plain[:, 0:H], start=True, stop=True
-            )
-            nc.tensor.matmul(
-                out=plain_ps[:, H:GATES], lhsT=state_t[:, j, 0, :], rhs=w_plain[:, H:GATES], start=True, stop=True
-            )
+            for cols, source in ((slice(0, H), 1), (slice(H, GATES), 0)):
+                if scalar_empties:
+                    nc.tensor.matmul(
+                        out=plain_ps[:, cols], lhsT=ones_bf[:], rhs=bias_row[:, cols], start=True, stop=False
+                    )
+                nc.tensor.matmul(
+                    out=plain_ps[:, cols],
+                    lhsT=state_t[:, j, source, :],
+                    rhs=w_plain[:, cols],
+                    start=not scalar_empties,
+                    stop=True,
+                )
             plain_sb = sums.tile([P, GATES], F32)
-            nc.vector.tensor_tensor(out=plain_sb[:], in0=plain_ps[:], in1=bias_f32[:], op=ALU.add)
+            if scalar_empties:
+                nc.scalar.copy(out=plain_sb[:], in_=plain_ps[:])
+            else:
+                nc.vector.tensor_tensor(out=plain_sb[:], in0=plain_ps[:], in1=bias_f32[:], op=ALU.add)
             plain_tiles[rnd * TILES_PER_ROUND + i] = plain_sb
 
         def mx_products(rnd):
@@ -299,8 +310,11 @@ def tile_multiinputlstmcell_pa_t_kernel(
             engine.tensor_tensor(
                 out=step[:, rows, :], in0=tail_tile("w_i", chunk)[:, rows, :], in1=tail_tile("g_minus_c", chunk)[:, rows, :], op=ALU.mult
             )
+
+        def cell(chunk, rows):
+            step = tail_tile("step", chunk)
             c_1 = tail_tile("c_1", chunk)
-            engine.tensor_tensor(out=c_1[:, rows, :], in0=step[:, rows, :], in1=c_tiles[chunk][:, rows, :], op=ALU.add)
+            nc.vector.tensor_tensor(out=c_1[:, rows, :], in0=step[:, rows, :], in1=c_tiles[chunk][:, rows, :], op=ALU.add)
             nc.sync.dma_start(out=c1_rows[chunk][:, rows, :], in_=c_1[:, rows, :])
 
         def cell_tanh(chunk, rows):
@@ -343,6 +357,9 @@ def tile_multiinputlstmcell_pa_t_kernel(
             transpose_state(s + STATE_AHEAD)
             if s == -STATE_AHEAD:
                 spread_biases()
+            if phase == 1:
+                for where in whole(chunk - 1):
+                    cell(*where)
             if phase == 0:
                 for where in whole(chunk - 3):
                     hidden(*where)
@@ -355,6 +372,7 @@ def tile_multiinputlstmcell_pa_t_kernel(
                 pair_weight(*where)
             for where in part(s - 2):
                 blend(*where, nc.vector)
+                cell(*where)
             for where in part(s - 3):
                 cell_tanh(*where)
             for where in part(s - 4):

@@ -172,7 +172,7 @@ def tile_multiinputlstmcell_pa_t_kernel(
                 nc.tensor.transpose(state_ps[:, j, 1, :], c_tiles[chunk][:, j, :], ident_bf[:])
             if half == ROUNDS_PER_CHUNK - 1:
                 state_t = chunks.tile([P, TILES_PER_CHUNK, 2, P], BF16)
-                nc.scalar.copy(out=state_t[:], in_=state_ps[:])
+                nc.scalar.copy(out=state_t[:].bitcast(F32), in_=state_ps[:].bitcast(F32))
                 state_t_tiles[chunk] = state_t
 
         def spread_biases():
@@ -358,19 +358,19 @@ def tile_multiinputlstmcell_pa_t_kernel(
             if s == -STATE_AHEAD:
                 spread_biases()
             if phase == 1:
+                for where in whole(chunk - 2):
+                    hidden(*where)
                 for where in whole(chunk - 1):
                     cell(*where)
             if phase == 0:
-                for where in whole(chunk - 3):
-                    hidden(*where)
                 for where in whole(chunk - 1):
                     blend_inputs(*where, nc.gpsimd)
                 for where in whole(chunk - 2):
                     cell_tanh(*where)
             for where in part(s - 1):
                 blend_inputs(*where, nc.vector)
-                pair_weight(*where)
             for where in part(s - 2):
+                pair_weight(*where)
                 blend(*where, nc.vector)
                 cell(*where)
             for where in part(s - 3):

@@ -90,15 +90,16 @@ def tile_multiinputlstmcell_pa_t_kernel(
             h_tiles[chunk] = h_sb
             c_tiles[chunk] = c_sb
 
-        def load_x(chunk, pieces=1):
+        def load_x(chunk, half=None):
             if chunk >= CHUNKS:
                 return
-            x_sb = loads.tile([P, TILES_PER_CHUNK, IN], BF16)
-            size = TILES_PER_CHUNK // pieces
-            for piece in range(pieces):
-                rows = slice(piece * size, (piece + 1) * size)
-                nc.sync.dma_start(out=x_sb[:, rows, :], in_=x_rows[chunk][:, rows, :])
-            x_tiles[chunk] = x_sb
+            if chunk not in x_tiles:
+                x_sb = loads.tile([P, TILES_PER_CHUNK, IN], BF16)
+                x_tiles[chunk] = x_sb
+            rows = slice(0, TILES_PER_CHUNK)
+            if half is not None:
+                rows = slice(half * TILES_PER_ROUND, (half + 1) * TILES_PER_ROUND)
+            nc.sync.dma_start(out=x_tiles[chunk][:, rows, :], in_=x_rows[chunk][:, rows, :])
 
         bias_row = consts.tile([P, GATES], BF16)
         nc.vector.memset(bias_row[:], 0.0)
@@ -108,9 +109,10 @@ def tile_multiinputlstmcell_pa_t_kernel(
         load_state(0)
         nc.sync.dma_start(out=bias_row[0:1, 0:H], in_=alpha_bias.unsqueeze(0))
         nc.sync.dma_start(out=bias_row[0:1, H:GATES], in_=bias.unsqueeze(0))
-        load_x(0, pieces=ROUNDS_PER_CHUNK)
+        load_x(0, half=0)
+        load_x(0, half=1)
         load_state(1)
-        load_x(1)
+        load_x(1, half=0)
 
         w4_words = consts.tile([P, PASSES, 2 * GATES], U8, align_bytes=64)
         nc.sync.dma_start(
@@ -147,6 +149,7 @@ def tile_multiinputlstmcell_pa_t_kernel(
         make_identity(nc, ident_bf[:])
 
         load_state(2)
+        load_x(1, half=1)
         load_x(2)
         load_state(3)
 
@@ -367,11 +370,12 @@ def tile_multiinputlstmcell_pa_t_kernel(
                     blend_inputs(*where, nc.gpsimd)
                 for where in whole(chunk - 2):
                     cell_tanh(*where)
-            for where in part(s - 1):
-                blend_inputs(*where, nc.vector)
             for where in part(s - 2):
                 pair_weight(*where)
                 blend(*where, nc.vector)
+            for where in part(s - 1):
+                blend_inputs(*where, nc.vector)
+            for where in part(s - 2):
                 cell(*where)
             for where in part(s - 3):
                 cell_tanh(*where)

@@ -308,16 +308,16 @@ def tile_multiinputlstmcell_pa_t_kernel(
             w_i = tail_tile("w_i", chunk)
             nc.scalar.activation(out=w_i[:, rows, :], in_=tail_tile("i_minus_a", chunk)[:, rows, :], func=ACT.Sigmoid)
 
-        def blend(chunk, rows, engine):
+        def blend(chunk, rows):
             step = tail_tile("step", chunk)
-            engine.tensor_tensor(
+            nc.vector.tensor_tensor(
                 out=step[:, rows, :], in0=tail_tile("w_i", chunk)[:, rows, :], in1=tail_tile("g_minus_c", chunk)[:, rows, :], op=ALU.mult
             )
 
-        def cell(chunk, rows):
+        def cell(chunk, rows, engine):
             step = tail_tile("step", chunk)
             c_1 = tail_tile("c_1", chunk)
-            nc.vector.tensor_tensor(out=c_1[:, rows, :], in0=step[:, rows, :], in1=c_tiles[chunk][:, rows, :], op=ALU.add)
+            engine.tensor_tensor(out=c_1[:, rows, :], in0=step[:, rows, :], in1=c_tiles[chunk][:, rows, :], op=ALU.add)
             nc.sync.dma_start(out=c1_rows[chunk][:, rows, :], in_=c_1[:, rows, :])
 
         def cell_tanh(chunk, rows):
@@ -347,13 +347,12 @@ def tile_multiinputlstmcell_pa_t_kernel(
             if phase == 0 and chunk >= 0:
                 load_state(chunk + STATE_LOAD_AHEAD)
                 load_x(chunk + LOAD_AHEAD)
-            if phase == 1:
-                for where in whole(chunk - 1):
-                    pair_weight(*where)
-                    blend(*where, nc.gpsimd)
             gates(s - 1)
             quantise(s + 1)
             transpose_x(s + X_AHEAD)
+            if phase == 1:
+                for where in whole(chunk - 1):
+                    pair_weight(*where)
             plain_products(s + PLAIN_AHEAD, 0)
             mx_products(s)
             plain_products(s + PLAIN_AHEAD, 1)
@@ -364,7 +363,8 @@ def tile_multiinputlstmcell_pa_t_kernel(
                 for where in whole(chunk - 2):
                     hidden(*where)
                 for where in whole(chunk - 1):
-                    cell(*where)
+                    blend(*where)
+                    cell(*where, nc.gpsimd)
             if phase == 0:
                 for where in whole(chunk - 1):
                     blend_inputs(*where, nc.gpsimd)
@@ -372,11 +372,11 @@ def tile_multiinputlstmcell_pa_t_kernel(
                     cell_tanh(*where)
             for where in part(s - 2):
                 pair_weight(*where)
-                blend(*where, nc.vector)
+                blend(*where)
             for where in part(s - 1):
                 blend_inputs(*where, nc.vector)
             for where in part(s - 2):
-                cell(*where)
+                cell(*where, nc.vector)
             for where in part(s - 3):
                 cell_tanh(*where)
             for where in part(s - 4):

@@ -37,7 +37,7 @@ PLAIN_AHEAD = 2
 STATE_AHEAD = 4
 CHUNKS_ENDING_ON_VECTOR = 2
 FIRST_ON_VECTOR = CHUNKS - CHUNKS_ENDING_ON_VECTOR
-TILE_ON_SCALAR = TILES_PER_CHUNK - 1
+TILE_ON_SCALAR = TILES_PER_CHUNK - 2
 
 FLOPS = 2 * BATCH * (IN + H) * GATES
 
@@ -293,15 +293,20 @@ def tile_multiinputlstmcell_pa_t_kernel(
                 tail_tiles[(name, chunk)] = tail
             return tail_tiles[(name, chunk)]
 
-        def blend_inputs(chunk, rows, engine):
+        def gate_difference(chunk, rows, engine):
             gate = gate_tiles[chunk]
             i_minus_a = tail_tile("i_minus_a", chunk)
             engine.tensor_tensor(
                 out=i_minus_a[:, rows, :], in0=gate[:, rows, H : 2 * H], in1=gate[:, rows, 0:H], op=ALU.subtract
             )
+
+        def cell_difference(chunk, rows, engine):
             g_minus_c = tail_tile("g_minus_c", chunk)
             engine.tensor_tensor(
-                out=g_minus_c[:, rows, :], in0=gate[:, rows, 3 * H : 4 * H], in1=c_tiles[chunk][:, rows, :], op=ALU.subtract
+                out=g_minus_c[:, rows, :],
+                in0=gate_tiles[chunk][:, rows, 3 * H : 4 * H],
+                in1=c_tiles[chunk][:, rows, :],
+                op=ALU.subtract,
             )
 
         def pair_weight(chunk, rows):
@@ -347,37 +352,46 @@ def tile_multiinputlstmcell_pa_t_kernel(
             if phase == 0 and chunk >= 0:
                 load_state(chunk + STATE_LOAD_AHEAD)
                 load_x(chunk + LOAD_AHEAD)
-            gates(s - 1)
-            quantise(s + 1)
-            transpose_x(s + X_AHEAD)
             if phase == 1:
                 for where in whole(chunk - 1):
                     pair_weight(*where)
-            plain_products(s + PLAIN_AHEAD, 0)
-            mx_products(s)
-            plain_products(s + PLAIN_AHEAD, 1)
-            transpose_state(s + STATE_AHEAD)
-            if s == -STATE_AHEAD:
-                spread_biases()
+            quantise(s + 1)
+            for where in part(s - 2):
+                pair_weight(*where)
             if phase == 1:
-                for where in whole(chunk - 2):
-                    hidden(*where)
                 for where in whole(chunk - 1):
                     blend(*where)
+            gates(s - 1)
+            if phase == 1:
+                for where in whole(chunk - 1):
                     cell(*where, nc.gpsimd)
+            transpose_x(s + X_AHEAD)
             if phase == 0:
                 for where in whole(chunk - 1):
-                    blend_inputs(*where, nc.gpsimd)
+                    gate_difference(*where, nc.gpsimd)
+            plain_products(s + PLAIN_AHEAD, 0)
+            mx_products(s)
+            if phase == 0:
                 for where in whole(chunk - 2):
                     cell_tanh(*where)
             for where in part(s - 2):
-                pair_weight(*where)
                 blend(*where)
-            for where in part(s - 1):
-                blend_inputs(*where, nc.vector)
-            for where in part(s - 2):
-                cell(*where, nc.vector)
-            for where in part(s - 3):
-                cell_tanh(*where)
             for where in part(s - 4):
                 hidden(*where)
+            plain_products(s + PLAIN_AHEAD, 1)
+            for where in part(s - 1):
+                gate_difference(*where, nc.vector)
+                cell_difference(*where, nc.vector)
+            transpose_state(s + STATE_AHEAD)
+            if s == -STATE_AHEAD:
+                spread_biases()
+            for where in part(s - 3):
+                cell_tanh(*where)
+            for where in part(s - 2):
+                cell(*where, nc.vector)
+            if phase == 0:
+                for where in whole(chunk - 1):
+                    cell_difference(*where, nc.gpsimd)
+            if phase == 1:
+                for where in whole(chunk - 2):
+                    hidden(*where)

from contextlib import ExitStack

import concourse.mybir as mybir
from concourse.masks import make_identity

F32 = mybir.dt.float32
BF16 = mybir.dt.bfloat16
I32 = mybir.dt.int32
U32 = mybir.dt.uint32
U8 = mybir.dt.uint8
FP8X4 = mybir.dt.float8_e4m3fn_x4
FP4X4 = mybir.dt.float4_e2m1fn_x4
ACT = mybir.ActivationFunctionType
ALU = mybir.AluOpType

P = 128
BATCH = 8192
IN = 1024
H = 128
GATES = 4 * H
SIGMOID_COLS = 3 * H
PACK = 4
K_PASS = P * PACK
PASSES = IN // K_PASS
WORD_HALVES = 2

ROW_TILES = BATCH // P
TILES_PER_ROUND = 2
ROUNDS = ROW_TILES // TILES_PER_ROUND
ROUNDS_PER_CHUNK = 2
TILES_PER_CHUNK = TILES_PER_ROUND * ROUNDS_PER_CHUNK
CHUNKS = ROW_TILES // TILES_PER_CHUNK
LOAD_AHEAD = 3
STATE_LOAD_AHEAD = 4
X_AHEAD = 2
PLAIN_AHEAD = 2
STATE_AHEAD = 4
CHUNKS_ENDING_ON_VECTOR = 2
FIRST_ON_VECTOR = CHUNKS - CHUNKS_ENDING_ON_VECTOR
TILE_ON_SCALAR = TILES_PER_CHUNK - 2

FLOPS = 2 * BATCH * (IN + H) * GATES


def tile_multiinputlstmcell_pa_t_kernel(
    tc,
    input_,
    c_input,
    h_0,
    weight_ih_words,
    weight_ih_scales,
    weight_hh,
    alpha_weight_ih_words,
    alpha_weight_ih_scales,
    alpha_weight_hh,
    bias,
    alpha_bias,
    out_0,
    out_1,
):
    nc = tc.nc
    x_rows = input_.rearrange("(c p j) k -> c p j k", p=P, j=TILES_PER_CHUNK)
    h_rows = h_0.rearrange("(c p j) h -> c p j h", p=P, j=TILES_PER_CHUNK)
    c_rows = c_input.rearrange("(c p j) o h -> c p j (o h)", p=P, j=TILES_PER_CHUNK)
    h1_rows = out_0.rearrange("(c p j) h -> c p j h", p=P, j=TILES_PER_CHUNK)
    c1_rows = out_1.rearrange("(c p j) h -> c p j h", p=P, j=TILES_PER_CHUNK)

    with ExitStack() as ctx:
        consts = ctx.enter_context(tc.tile_pool(name="consts", bufs=1))
        loads = ctx.enter_context(tc.tile_pool(name="loads", bufs=LOAD_AHEAD + 1))
        hiddens = ctx.enter_context(tc.tile_pool(name="hiddens", bufs=STATE_LOAD_AHEAD + 1))
        cells = ctx.enter_context(tc.tile_pool(name="cells", bufs=STATE_LOAD_AHEAD + 4))
        rounds = ctx.enter_context(tc.tile_pool(name="rounds", bufs=X_AHEAD + 1))
        sums = ctx.enter_context(tc.tile_pool(name="sums", bufs=(PLAIN_AHEAD + 1) * TILES_PER_ROUND))
        chunks = ctx.enter_context(tc.tile_pool(name="chunks", bufs=4))
        psum = ctx.enter_context(tc.psum_pool(name="psum", bufs=2))
        ctx.enter_context(tc.manual_schedule())

        x_tiles = {}
        h_tiles = {}
        c_tiles = {}

        def load_state(chunk):
            if chunk >= CHUNKS:
                return
            h_sb = hiddens.tile([P, TILES_PER_CHUNK, H], BF16)
            nc.sync.dma_start(out=h_sb[:], in_=h_rows[chunk])
            c_sb = cells.tile([P, TILES_PER_CHUNK, H], BF16)
            nc.sync.dma_start(out=c_sb[:], in_=c_rows[chunk])
            h_tiles[chunk] = h_sb
            c_tiles[chunk] = c_sb

        def load_x(chunk, half=None):
            if chunk >= CHUNKS:
                return
            if chunk not in x_tiles:
                x_sb = loads.tile([P, TILES_PER_CHUNK, IN], BF16)
                x_tiles[chunk] = x_sb
            rows = slice(0, TILES_PER_CHUNK)
            if half is not None:
                rows = slice(half * TILES_PER_ROUND, (half + 1) * TILES_PER_ROUND)
            nc.sync.dma_start(out=x_tiles[chunk][:, rows, :], in_=x_rows[chunk][:, rows, :])

        bias_row = consts.tile([P, GATES], BF16)
        nc.vector.memset(bias_row[:], 0.0)
        ones_bf = consts.tile([P, P], BF16)
        nc.vector.memset(ones_bf[:], 1.0)

        load_state(0)
        nc.sync.dma_start(out=bias_row[0:1, 0:H], in_=alpha_bias.unsqueeze(0))
        nc.sync.dma_start(out=bias_row[0:1, H:GATES], in_=bias.unsqueeze(0))
        load_x(0, half=0)
        load_x(0, half=1)
        load_state(1)
        load_x(1, half=0)

        w4_words = consts.tile([P, PASSES, 2 * GATES], U8, align_bytes=64)
        nc.sync.dma_start(
            out=w4_words[:, :, 0 : 2 * H].bitcast(I32),
            in_=alpha_weight_ih_words.rearrange("g p n -> p g n").bitcast(I32),
        )
        nc.sync.dma_start(
            out=w4_words[:, :, 2 * H : 2 * GATES].bitcast(I32),
            in_=weight_ih_words.rearrange("g p n -> p g n").bitcast(I32),
        )
        w4_scales = consts.tile([P, PASSES, GATES], U8, align_bytes=64)
        nc.vector.memset(w4_scales[:].bitcast(I32), 0)
        for quadrant in range(4):
            live = slice(32 * quadrant, 32 * quadrant + 4)
            given = slice(4 * quadrant, 4 * quadrant + 4)
            nc.sync.dma_start(
                out=w4_scales[live, :, 0:H].bitcast(I32),
                in_=alpha_weight_ih_scales[:, given, :].rearrange("g r n -> r g n").bitcast(I32),
            )
            nc.sync.dma_start(
                out=w4_scales[live, :, H:GATES].bitcast(I32),
                in_=weight_ih_scales[:, given, :].rearrange("g r n -> r g n").bitcast(I32),
            )
        w_plain = consts.tile([P, GATES], BF16)
        nc.scalar.dma_start(out=w_plain[:, 0:H], in_=alpha_weight_hh)
        nc.scalar.dma_start(out=w_plain[:, H:GATES], in_=weight_hh)
        bias_f32 = consts.tile([P, GATES], F32)
        warm = consts.tile([P, 2], F32)
        nc.vector.memset(warm[:], 0.0)
        nc.scalar.activation(out=warm[:, 1:2], in_=warm[:, 0:1], func=ACT.Sigmoid)
        ident_f32 = consts.tile([P, P], F32)
        make_identity(nc, ident_f32[:])
        ident_bf = consts.tile([P, P], BF16)
        make_identity(nc, ident_bf[:])

        load_state(2)
        load_x(1, half=1)
        load_x(2)
        load_state(3)

        state_banks = {}
        state_t_tiles = {}
        grouped_tiles = {}
        code_tiles = {}
        plain_tiles = {}
        pre_tiles = {}
        gate_tiles = {}
        tail_tiles = {}

        def transpose_state(rnd):
            if not 0 <= rnd < ROUNDS:
                return
            chunk, half = divmod(rnd, ROUNDS_PER_CHUNK)
            if half == 0:
                state_ps = psum.tile([P, TILES_PER_CHUNK, 2, P], BF16)
                state_banks[chunk] = state_ps
            state_ps = state_banks[chunk]
            for j in range(half * TILES_PER_ROUND, (half + 1) * TILES_PER_ROUND):
                nc.tensor.transpose(state_ps[:, j, 0, :], h_tiles[chunk][:, j, :], ident_bf[:])
                nc.tensor.transpose(state_ps[:, j, 1, :], c_tiles[chunk][:, j, :], ident_bf[:])
            if half == ROUNDS_PER_CHUNK - 1:
                state_t = chunks.tile([P, TILES_PER_CHUNK, 2, P], BF16)
                nc.scalar.copy(out=state_t[:].bitcast(F32), in_=state_ps[:].bitcast(F32))
                state_t_tiles[chunk] = state_t

        def spread_biases():
            plain_ps = psum.tile([P, GATES], F32)
            nc.tensor.matmul(out=plain_ps[:], lhsT=ones_bf[:], rhs=bias_row[:], start=True, stop=True)
            nc.vector.tensor_copy(out=bias_f32[:], in_=plain_ps[:])

        def transpose_x(rnd):
            if not 0 <= rnd < ROUNDS:
                return
            chunk, half = divmod(rnd, ROUNDS_PER_CHUNK)
            x_words = x_tiles[chunk][:].bitcast(F32)
            grouped = rounds.tile([P, TILES_PER_ROUND, PASSES, P, PACK], BF16, align_bytes=64)
            grouped_words = grouped[:].bitcast(F32)
            for i in range(TILES_PER_ROUND):
                j = half * TILES_PER_ROUND + i
                x_ps = psum.tile([P, PASSES, WORD_HALVES, P], F32)
                for g in range(PASSES):
                    for u in range(WORD_HALVES):
                        first = g * P * WORD_HALVES + u
                        last = (g + 1) * P * WORD_HALVES
                        nc.tensor.transpose(
                            x_ps[:, g, u, :], x_words[:, j, first:last:WORD_HALVES], ident_f32[:]
                        )
                nc.scalar.copy(out=grouped_words[:, i], in_=x_ps[:].rearrange("p g u b -> p g b u"))
            grouped_tiles[rnd] = grouped

        def quantise(rnd):
            if not 0 <= rnd < ROUNDS:
                return
            codes = rounds.tile([P, TILES_PER_ROUND, PASSES, P], U32, align_bytes=64)
            scales = rounds.tile([P, TILES_PER_ROUND, PASSES, P], U8, align_bytes=64)
            nc.vector.quantize_mx(
                out=codes[:].rearrange("p i g b -> p (i g b)").bitcast(FP8X4),
                scales=scales[:].rearrange("p i g b -> p (i g b)"),
                in_=grouped_tiles[rnd][:].rearrange("p i g b t -> p (i g b t)"),
            )
            code_tiles[rnd] = (codes, scales)

        def plain_products(rnd, i):
            if not 0 <= rnd < ROUNDS:
                return
            chunk, half = divmod(rnd, ROUNDS_PER_CHUNK)
            state_t = state_t_tiles[chunk]
            j = half * TILES_PER_ROUND + i
            scalar_empties = j == TILE_ON_SCALAR
            plain_ps = psum.tile([P, GATES], F32)
            for cols, source in ((slice(0, H), 1), (slice(H, GATES), 0)):
                if scalar_empties:
                    nc.tensor.matmul(
                        out=plain_ps[:, cols], lhsT=ones_bf[:], rhs=bias_row[:, cols], start=True, stop=False
                    )
                nc.tensor.matmul(
                    out=plain_ps[:, cols],
                    lhsT=state_t[:, j, source, :],
                    rhs=w_plain[:, cols],
                    start=not scalar_empties,
                    stop=True,
                )
            plain_sb = sums.tile([P, GATES], F32)
            if scalar_empties:
                nc.scalar.copy(out=plain_sb[:], in_=plain_ps[:])
            else:
                nc.vector.tensor_tensor(out=plain_sb[:], in0=plain_ps[:], in1=bias_f32[:], op=ALU.add)
            plain_tiles[rnd * TILES_PER_ROUND + i] = plain_sb

        def mx_products(rnd):
            if not 0 <= rnd < ROUNDS:
                return
            chunk, half = divmod(rnd, ROUNDS_PER_CHUNK)
            if half == 0:
                pre = chunks.tile([P, TILES_PER_CHUNK, GATES], F32)
                pre_tiles[chunk] = pre
            codes, scales = code_tiles[rnd]
            for i in range(TILES_PER_ROUND):
                j = half * TILES_PER_ROUND + i
                mx_ps = psum.tile([P, GATES], F32)
                for g in range(PASSES):
                    nc.tensor.matmul_mx(
                        out=mx_ps[:],
                        lhsT=codes[:, i, g, :].bitcast(FP8X4),
                        lhsT_scale=scales[:, i, g, :],
                        rhs=w4_words[:, g, :].bitcast(FP4X4),
                        rhs_scale=w4_scales[:, g, :],
                        start=(g == 0),
                        stop=(g == PASSES - 1),
                    )
                nc.vector.tensor_tensor(
                    out=pre_tiles[chunk][:, j, :],
                    in0=mx_ps[:],
                    in1=plain_tiles[rnd * TILES_PER_ROUND + i][:],
                    op=ALU.add,
                )

        def gates(rnd):
            if not 0 <= rnd < ROUNDS:
                return
            chunk, half = divmod(rnd, ROUNDS_PER_CHUNK)
            if half == 0:
                gate = chunks.tile([P, TILES_PER_CHUNK, GATES], F32)
                gate_tiles[chunk] = gate
            rows = slice(half * TILES_PER_ROUND, (half + 1) * TILES_PER_ROUND)
            pre = pre_tiles[chunk]
            gate = gate_tiles[chunk]
            nc.scalar.activation(
                out=gate[:, rows, 0:SIGMOID_COLS], in_=pre[:, rows, 0:SIGMOID_COLS], func=ACT.Sigmoid
            )
            nc.scalar.activation(
                out=gate[:, rows, SIGMOID_COLS:GATES], in_=pre[:, rows, SIGMOID_COLS:GATES], func=ACT.Tanh
            )

        def tail_tile(name, chunk):
            if (name, chunk) not in tail_tiles:
                tail = chunks.tile([P, TILES_PER_CHUNK, H], F32, name=name)
                tail_tiles[(name, chunk)] = tail
            return tail_tiles[(name, chunk)]

        def gate_difference(chunk, rows, engine):
            gate = gate_tiles[chunk]
            i_minus_a = tail_tile("i_minus_a", chunk)
            engine.tensor_tensor(
                out=i_minus_a[:, rows, :], in0=gate[:, rows, H : 2 * H], in1=gate[:, rows, 0:H], op=ALU.subtract
            )

        def cell_difference(chunk, rows, engine):
            g_minus_c = tail_tile("g_minus_c", chunk)
            engine.tensor_tensor(
                out=g_minus_c[:, rows, :],
                in0=gate_tiles[chunk][:, rows, 3 * H : 4 * H],
                in1=c_tiles[chunk][:, rows, :],
                op=ALU.subtract,
            )

        def pair_weight(chunk, rows):
            w_i = tail_tile("w_i", chunk)
            nc.scalar.activation(out=w_i[:, rows, :], in_=tail_tile("i_minus_a", chunk)[:, rows, :], func=ACT.Sigmoid)

        def blend(chunk, rows):
            step = tail_tile("step", chunk)
            nc.vector.tensor_tensor(
                out=step[:, rows, :], in0=tail_tile("w_i", chunk)[:, rows, :], in1=tail_tile("g_minus_c", chunk)[:, rows, :], op=ALU.mult
            )

        def cell(chunk, rows, engine):
            step = tail_tile("step", chunk)
            c_1 = tail_tile("c_1", chunk)
            engine.tensor_tensor(out=c_1[:, rows, :], in0=step[:, rows, :], in1=c_tiles[chunk][:, rows, :], op=ALU.add)
            nc.sync.dma_start(out=c1_rows[chunk][:, rows, :], in_=c_1[:, rows, :])

        def cell_tanh(chunk, rows):
            tanh_c1 = tail_tile("tanh_c1", chunk)
            nc.scalar.activation(out=tanh_c1[:, rows, :], in_=tail_tile("c_1", chunk)[:, rows, :], func=ACT.Tanh)

        def hidden(chunk, rows):
            h_1 = tail_tile("h_1", chunk)
            nc.vector.tensor_tensor(
                out=h_1[:, rows, :],
                in0=gate_tiles[chunk][:, rows, 2 * H : 3 * H],
                in1=tail_tile("tanh_c1", chunk)[:, rows, :],
                op=ALU.mult,
            )
            nc.sync.dma_start(out=h1_rows[chunk][:, rows, :], in_=h_1[:, rows, :])

        def whole(chunk):
            return [(chunk, slice(0, TILES_PER_CHUNK))] if 0 <= chunk < FIRST_ON_VECTOR else []

        def part(rnd):
            chunk, half = divmod(rnd, ROUNDS_PER_CHUNK)
            rows = slice(half * TILES_PER_ROUND, (half + 1) * TILES_PER_ROUND)
            return [(chunk, rows)] if FIRST_ON_VECTOR <= chunk < CHUNKS else []

        for s in range(-STATE_AHEAD, ROUNDS + 2 * ROUNDS_PER_CHUNK + 1):
            chunk, phase = divmod(s, ROUNDS_PER_CHUNK)
            if phase == 0 and chunk >= 0:
                load_state(chunk + STATE_LOAD_AHEAD)
                load_x(chunk + LOAD_AHEAD)
            if phase == 1:
                for where in whole(chunk - 1):
                    pair_weight(*where)
            quantise(s + 1)
            for where in part(s - 2):
                pair_weight(*where)
            if phase == 1:
                for where in whole(chunk - 1):
                    blend(*where)
            gates(s - 1)
            if phase == 1:
                for where in whole(chunk - 1):
                    cell(*where, nc.gpsimd)
            transpose_x(s + X_AHEAD)
            if phase == 0:
                for where in whole(chunk - 1):
                    gate_difference(*where, nc.gpsimd)
            plain_products(s + PLAIN_AHEAD, 0)
            mx_products(s)
            if phase == 0:
                for where in whole(chunk - 2):
                    cell_tanh(*where)
            for where in part(s - 2):
                blend(*where)
            for where in part(s - 4):
                hidden(*where)
            plain_products(s + PLAIN_AHEAD, 1)
            for where in part(s - 1):
                gate_difference(*where, nc.vector)
                cell_difference(*where, nc.vector)
            transpose_state(s + STATE_AHEAD)
            if s == -STATE_AHEAD:
                spread_biases()
            for where in part(s - 3):
                cell_tanh(*where)
            for where in part(s - 2):
                cell(*where, nc.vector)
            if phase == 0:
                for where in whole(chunk - 1):
                    cell_difference(*where, nc.gpsimd)
            if phase == 1:
                for where in whole(chunk - 2):
                    hidden(*where)
